import numpy as np
import ml_dtypes


def mxq(x, axis, fmt="e4m3"):
    dtype, down = {"e4m3": (ml_dtypes.float8_e4m3fn, 7), "e5m2": (ml_dtypes.float8_e5m2, 14)}[fmt]
    v = np.moveaxis(np.asarray(x, np.float32).astype(ml_dtypes.bfloat16).astype(np.float64), axis, -1)
    blocks = v.reshape(v.shape[:-1] + (-1, 32))
    amax = np.abs(blocks).max(-1, keepdims=True)
    byte = np.maximum(np.where(amax > 0, np.frexp(amax)[1] - 1 + 127, 0) - down, 1)
    scale = np.exp2(byte - 127.0)
    codes = (blocks / scale).astype(np.float32).astype(dtype).astype(np.float64)
    return np.moveaxis((codes * scale).reshape(v.shape), -1, axis)


WIDE = False


def mx_kscale(k):
    if not WIDE:
        return np.ones(k)
    levels = np.array([18, -18])
    if k % 512:
        return np.exp2(np.random.permutation(np.resize(levels, k // 32))).repeat(32)
    a = np.empty((k // 512, 16))
    for p in range(k // 512):
        a[p, :8] = np.random.permutation(np.resize(levels, 8))
        for g in range(8):
            far = levels[np.abs(levels - a[p, g]) >= 10]
            a[p, g + 8] = far[np.random.randint(len(far))]
    return np.exp2(a.ravel()).repeat(32)


BF16 = ml_dtypes.bfloat16


def bf(x):
    return np.asarray(x, np.float32).astype(BF16)


def f64(x):
    return np.asarray(x).astype(np.float64)


B, S, H = 2, 512, 1536
M = B * S


def setup_inputs():
    s = mx_kscale(M).reshape(B, S, 1)
    u = mx_kscale(H)
    x0 = bf(np.random.standard_normal((B, S, H)))
    pw0 = bf(np.random.standard_normal((H, H)) / np.sqrt(H))
    rate = bf(np.random.uniform(0.2, 0.4, 1))
    fw0 = bf(np.random.standard_normal((H, H)) / np.sqrt(H))
    b = bf(np.random.standard_normal(H) * 0.3)
    hs = bf(np.random.uniform(1.5, 2.5, 1))
    g = bf(np.random.standard_normal((B, S, H)) * np.exp2(np.random.randint(-6, 1, (B, S, 1))) / s * u)
    return {"x": bf(f64(x0) * s),
            "plastic_weights": bf(f64(pw0) / u[:, None]),
            "plasticity_rate": rate,
            "fixed_w": bf(f64(fw0) / u[:, None]),
            "fixed_b": b,
            "hebbian_strength": hs,
            "grad_out": g}


def reference(x, plastic_weights, plasticity_rate, fixed_w, fixed_b, hebbian_strength, grad_out):
    xf = f64(x).reshape(M, H)
    g = f64(grad_out).reshape(M, H)
    w = f64(fixed_w) + f64(plastic_weights)
    dx = mxq(g, 1, "e5m2") @ mxq(w, 0, "e4m3")
    dw = mxq(g, 0, "e5m2").T @ mxq(xf, 0, "e4m3")
    return dx.reshape(B, S, H), dw

@@ -1,0 +1,249 @@
+from contextlib import ExitStack
+
+import concourse.mybir as mybir
+from concourse.masks import make_identity
+
+F32 = mybir.dt.float32
+BF16 = mybir.dt.bfloat16
+U32 = mybir.dt.uint32
+U8 = mybir.dt.uint8
+E4M3X4 = mybir.dt.float8_e4m3fn_x4
+E5M2X4 = mybir.dt.float8_e5m2_x4
+
+P = 128
+PACK = 4
+K_PASS = P * PACK
+TOKENS = 1024
+H = 1536
+N = 512
+TOKEN_PASSES = TOKENS // K_PASS
+FEATURE_PASSES = H // K_PASS
+BLOCKS = H // N
+RUN = 4
+
+FLOPS = 2 * 2 * TOKENS * H * H
+BYTES = 2 * (2 * TOKENS * H + 2 * H * H) + 4 * (TOKENS * H + H * H)
+
+
+def tile_neuroplasticitylayer_v_kernel(
+    tc, x, plastic_weights, plasticity_rate, fixed_w, fixed_b, hebbian_strength, grad_out, out_0, out_1
+):
+    nc = tc.nc
+    with ExitStack() as ctx:
+        keep = ctx.enter_context(tc.tile_pool(name="keep", bufs=1))
+        stage = ctx.enter_context(tc.tile_pool(name="stage", bufs=9))
+        psum = ctx.enter_context(tc.psum_pool(name="psum", bufs=8))
+        ctx.enter_context(tc.manual_schedule())
+
+        def big(slot, shape, dtype):
+            return keep.tile(shape, dtype, tag="big%d" % slot, name="big%d" % slot, align_bytes=64)
+
+        def load_pass(rows, slot, pieces=1):
+            raw = big(slot, [P, PACK * H], BF16)
+            view = rows.rearrange("(p j) w -> p (j w)", j=PACK)
+            width = PACK * H // pieces
+            for piece in range(pieces):
+                cols = slice(piece * width, (piece + 1) * width)
+                nc.sync.dma_start(out=raw[:, cols], in_=view[:, cols])
+            return raw
+
+        def staged(name):
+            return stage.tile([P, PACK * N], BF16, tag="staged", name=name, align_bytes=64)
+
+        def block_of(raw, block):
+            return raw[:].rearrange("p (j w) -> p j w", j=PACK)[:, :, block * N:(block + 1) * N]
+
+        def copy(on_scalar, out, in_):
+            if on_scalar:
+                nc.scalar.copy(out=out, in_=in_)
+            else:
+                nc.vector.tensor_copy(out=out, in_=in_)
+
+        def interleave(rows, on_scalar=False):
+            grouped = staged("grouped")
+            copy(
+                on_scalar,
+                grouped[:].rearrange("p (c i t) -> p c t i", i=RUN, t=PACK),
+                rows.rearrange("p t (c i) -> p c t i", i=RUN),
+            )
+            return grouped
+
+        def quantize(grouped, operand, block):
+            codes, scales, fmt = operand
+            cols = slice(block * N, (block + 1) * N)
+            nc.vector.quantize_mx(out=codes[:, cols].bitcast(fmt), scales=scales[:, cols], in_=grouped[:])
+
+        def scale_tile(name, width):
+            return keep.tile([P, width], U8, tag=name, name=name, align_bytes=64)
+
+        def product(passes, m, block, result, on_scalar=True):
+            acc = psum.tile([P, N], F32, tag="bank", name="acc")
+            m_cols = slice(m * P, (m + 1) * P)
+            n_cols = slice(block * N, (block + 1) * N)
+            for index, (left, right) in enumerate(passes):
+                nc.tensor.matmul_mx(
+                    out=acc[:],
+                    lhsT=left[0][:, m_cols].bitcast(left[2]),
+                    lhsT_scale=left[1][:, m_cols],
+                    rhs=right[0][:, n_cols].bitcast(right[2]),
+                    rhs_scale=right[1][:, n_cols],
+                    start=(index == 0),
+                    stop=(index == len(passes) - 1),
+                )
+            copy(on_scalar, result, acc[:])
+
+        g_raw = [load_pass(grad_out[0], 0, pieces=2), load_pass(grad_out[1], 1)]
+        x_raw = [load_pass(x[0], 2), load_pass(x[1], 3)]
+        w_raw = {}
+
+        def load_weights(h, slots):
+            rows = slice(h * K_PASS, (h + 1) * K_PASS)
+            w_raw[h] = (load_pass(fixed_w[rows, :], slots[0]), load_pass(plastic_weights[rows, :], slots[1]))
+
+        load_weights(0, (4, 5))
+
+        identity = keep.tile([P, P], F32, name="identity")
+        make_identity(nc, identity[:])
+
+        g_codes = big(6, [P, TOKEN_PASSES * H], U32)
+        x_codes = big(7, [P, TOKEN_PASSES * H], U32)
+        g_tok = [(g_codes[:, g * H:(g + 1) * H], scale_tile("g_tok_s%d" % g, H), E5M2X4) for g in range(TOKEN_PASSES)]
+        x_tok = [(x_codes[:, g * H:(g + 1) * H], scale_tile("x_tok_s%d" % g, H), E4M3X4) for g in range(TOKEN_PASSES)]
+        g_feat = [
+            (keep.tile([P, TOKENS], U32, name="g_feat%d" % h, align_bytes=64), scale_tile("g_feat_s%d" % h, TOKENS), E5M2X4)
+            for h in range(FEATURE_PASSES)
+        ]
+        w_q = [
+            (keep.tile([P, H], U32, name="w_q%d" % h, align_bytes=64), scale_tile("w_q_s%d" % h, H), E4M3X4)
+            for h in range(FEATURE_PASSES)
+        ]
+
+        def transpose_pass(g):
+            words = g_raw[g][:].bitcast(F32)
+            grouped = [staged("turned") for h in range(FEATURE_PASSES)]
+            for pair in range(2):
+                for h in range(FEATURE_PASSES):
+                    bank = psum.tile([P, 2, 2, P], F32, tag="bank", name="turn")
+                    for a in range(2):
+                        first = (2 * pair + a) * (H // 2) + h * (K_PASS // 2)
+                        for u in range(2):
+                            nc.tensor.transpose(bank[:, a, u, :], words[:, first + u:first + K_PASS // 2:2], identity[:])
+                    half = grouped[h][:].bitcast(F32)[:, pair * N:(pair + 1) * N]
+                    nc.scalar.copy(
+                        out=half.rearrange("p (a r u) -> p a r u", a=2, u=2),
+                        in_=bank[:].rearrange("p a u r -> p a r u"),
+                    )
+            return grouped
+
+        def add_weights(h, block):
+            total = staged("total")
+            rows = total[:].rearrange("p (j w) -> p j w", j=PACK)
+            nc.vector.tensor_add(out=rows, in0=block_of(w_raw[h][0], block), in1=block_of(w_raw[h][1], block))
+            return rows
+
+        turned0 = transpose_pass(0)
+        g00 = interleave(block_of(g_raw[0], 0))
+        g02 = interleave(block_of(g_raw[0], 2))
+        g01 = interleave(block_of(g_raw[0], 1), on_scalar=True)
+        quantize(g00, g_tok[0], 0)
+        g10 = interleave(block_of(g_raw[1], 0))
+        turned1 = transpose_pass(1)
+        quantize(g02, g_tok[0], 2)
+        for h in range(FEATURE_PASSES):
+            quantize(turned0[h], g_feat[h], 0)
+        quantize(g10, g_tok[1], 0)
+        x00 = interleave(block_of(x_raw[0], 0))
+        x01 = interleave(block_of(x_raw[0], 1))
+        x02 = interleave(block_of(x_raw[0], 2), on_scalar=True)
+        quantize(x00, x_tok[0], 0)
+        x10 = interleave(block_of(x_raw[1], 0))
+        x11 = interleave(block_of(x_raw[1], 1), on_scalar=True)
+        quantize(x01, x_tok[0], 1)
+        quantize(x10, x_tok[1], 0)
+        x12 = interleave(block_of(x_raw[1], 2))
+        load_weights(1, (2, 3))
+        quantize(x11, x_tok[1], 1)
+        quantize(x02, x_tok[0], 2)
+        quantize(x12, x_tok[1], 2)
+        g11 = interleave(block_of(g_raw[1], 1))
+        quantize(g01, g_tok[0], 1)
+        g12 = interleave(block_of(g_raw[1], 2))
+        load_weights(2, (0, 1))
+        quantize(g11, g_tok[1], 1)
+        quantize(turned1[0], g_feat[0], 1)
+        quantize(g12, g_tok[1], 2)
+        quantize(turned1[1], g_feat[1], 1)
+        quantize(turned1[2], g_feat[2], 1)
+
+        dw_passes = list(zip(g_tok, x_tok))
+        dw_rows = out_1.rearrange("(q a p) w -> q p a w", a=2, p=P)
+
+        def dw_cols(tile, a, block):
+            return tile[:, a * H + block * N:a * H + (block + 1) * N]
+
+        def store_dw(q, tile):
+            nc.sync.dma_start(out=dw_rows[q], in_=tile[:].rearrange("p (a w) -> p a w", a=2))
+
+        first = [big(8 + q, [P, 2 * H], F32) for q in range(2)]
+        for block in range(BLOCKS):
+            for m in range(4):
+                product(dw_passes, m, block, dw_cols(first[m // 2], m % 2, block))
+        for q in range(2):
+            store_dw(q, first[q])
+
+        def dw_pair(q, slot):
+            tile = big(slot, [P, 2 * H], F32)
+            for a in range(2):
+                for block in range(BLOCKS):
+                    product(dw_passes, 2 * q + a, block, dw_cols(tile, a, block))
+            store_dw(q, tile)
+
+        for q in range(2, 5):
+            dw_pair(q, 8 + q)
+
+        s00 = add_weights(0, 0)
+        s01 = add_weights(0, 1)
+        w00 = interleave(s00)
+        s02 = add_weights(0, 2)
+        dw_pair(5, 4)
+        quantize(w00, w_q[0], 0)
+        s10 = add_weights(1, 0)
+        s11 = add_weights(1, 1)
+        w10 = interleave(s10)
+        s20 = add_weights(2, 0)
+        quantize(w10, w_q[1], 0)
+        w20 = interleave(s20)
+        w11 = interleave(s11)
+        quantize(w20, w_q[2], 0)
+
+        dx_passes = list(zip(g_feat, w_q))
+        dx_rows = out_0.rearrange("g (p j) w -> g p j w", j=PACK)
+
+        def dx_block(g, block, slot, shared=False):
+            tile = big(slot, [P, PACK * N], F32)
+            for j in range(PACK):
+                product(dx_passes, PACK * g + j, block, tile[:, j * N:(j + 1) * N], not shared or j % 2 == 0)
+            nc.sync.dma_start(
+                out=dx_rows[g][:, :, block * N:(block + 1) * N], in_=tile[:].rearrange("p (j w) -> p j w", j=PACK)
+            )
+
+        w01 = interleave(s01, on_scalar=True)
+        dx_block(0, 0, 5)
+        dx_block(1, 0, 6)
+        s21 = add_weights(2, 1)
+        quantize(w11, w_q[1], 1)
+        w21 = interleave(s21)
+        quantize(w01, w_q[0], 1)
+        s12 = add_weights(1, 2)
+        quantize(w21, w_q[2], 1)
+        w02 = interleave(s02, on_scalar=True)
+        dx_block(0, 1, 7)
+        dx_block(1, 1, 8)
+        w12 = interleave(s12)
+        s22 = add_weights(2, 2)
+        quantize(w12, w_q[1], 2)
+        w22 = interleave(s22)
+        quantize(w02, w_q[0], 2)
+        quantize(w22, w_q[2], 2)
+        dx_block(0, 2, 9, shared=True)
+        dx_block(1, 2, 10, shared=True)

@@ -170,10 +170,8 @@ def tile_neuroplasticitylayer_v_kernel(
         g12 = interleave(block_of(g_raw[1], 2))
         load_weights(2, (0, 1))
         quantize(g11, g_tok[1], 1)
-        quantize(turned1[0], g_feat[0], 1)
+        s00 = add_weights(0, 0)
         quantize(g12, g_tok[1], 2)
-        quantize(turned1[1], g_feat[1], 1)
-        quantize(turned1[2], g_feat[2], 1)
 
         dw_passes = list(zip(g_tok, x_tok))
         dw_rows = out_1.rearrange("(q a p) w -> q p a w", a=2, p=P)
@@ -201,49 +199,63 @@ def tile_neuroplasticitylayer_v_kernel(
         for q in range(2, 5):
             dw_pair(q, 8 + q)
 
-        s00 = add_weights(0, 0)
-        s01 = add_weights(0, 1)
         w00 = interleave(s00)
+        s01 = add_weights(0, 1)
+        quantize(w00, w_q[0], 0)
         s02 = add_weights(0, 2)
         dw_pair(5, 4)
-        quantize(w00, w_q[0], 0)
         s10 = add_weights(1, 0)
-        s11 = add_weights(1, 1)
+        quantize(turned1[0], g_feat[0], 1)
         w10 = interleave(s10)
-        s20 = add_weights(2, 0)
+        s11 = add_weights(1, 1)
         quantize(w10, w_q[1], 0)
+        s20 = add_weights(2, 0)
+        quantize(turned1[1], g_feat[1], 1)
         w20 = interleave(s20)
-        w11 = interleave(s11)
+        quantize(turned1[2], g_feat[2], 1)
         quantize(w20, w_q[2], 0)
 
         dx_passes = list(zip(g_feat, w_q))
-        dx_rows = out_0.rearrange("g (p j) w -> g p j w", j=PACK)
+        dx_rows = out_0.rearrange("g (p q a) w -> g q p a w", q=2, a=2)
+        dx_tiles = [big(5 + pair, [P, 2 * H], F32) for pair in range(4)]
 
-        def dx_block(g, block, slot, shared=False):
-            tile = big(slot, [P, PACK * N], F32)
-            for j in range(PACK):
-                product(dx_passes, PACK * g + j, block, tile[:, j * N:(j + 1) * N], not shared or j % 2 == 0)
+        def dx_block(pair, block, shared=False):
+            for a in range(2):
+                product(dx_passes, 2 * pair + a, block, dw_cols(dx_tiles[pair], a, block), not shared or a == 0)
+
+        def store_dx(pair, first, last):
+            cols = slice(first * N, last * N)
             nc.sync.dma_start(
-                out=dx_rows[g][:, :, block * N:(block + 1) * N], in_=tile[:].rearrange("p (j w) -> p j w", j=PACK)
+                out=dx_rows[pair // 2, pair % 2][:, :, cols],
+                in_=dx_tiles[pair][:].rearrange("p (a w) -> p a w", a=2)[:, :, cols],
             )
 
         w01 = interleave(s01, on_scalar=True)
-        dx_block(0, 0, 5)
-        dx_block(1, 0, 6)
+        dx_block(0, 0)
+        dx_block(1, 0)
+        w02 = interleave(s02, on_scalar=True)
+        dx_block(2, 0)
+        dx_block(3, 0)
         s21 = add_weights(2, 1)
-        quantize(w11, w_q[1], 1)
+        w11 = interleave(s11)
         w21 = interleave(s21)
         quantize(w01, w_q[0], 1)
-        s12 = add_weights(1, 2)
+        quantize(w11, w_q[1], 1)
         quantize(w21, w_q[2], 1)
-        w02 = interleave(s02, on_scalar=True)
-        dx_block(0, 1, 7)
-        dx_block(1, 1, 8)
-        w12 = interleave(s12)
+        for pair in range(2):
+            dx_block(pair, 1)
+            store_dx(pair, 0, 2)
+        s12 = add_weights(1, 2)
         s22 = add_weights(2, 2)
-        quantize(w12, w_q[1], 2)
+        w12 = interleave(s12)
         w22 = interleave(s22)
         quantize(w02, w_q[0], 2)
+        quantize(w12, w_q[1], 2)
         quantize(w22, w_q[2], 2)
-        dx_block(0, 2, 9, shared=True)
-        dx_block(1, 2, 10, shared=True)
+        for pair in range(2, 4):
+            dx_block(pair, 1, shared=pair == 3)
+            dx_block(pair, 2, shared=True)
+            store_dx(pair, 0, 3)
+        for pair in range(2):
+            dx_block(pair, 2, shared=True)
+            store_dx(pair, 2, 3)

from contextlib import ExitStack

import concourse.mybir as mybir
from concourse.masks import make_identity

F32 = mybir.dt.float32
BF16 = mybir.dt.bfloat16
U32 = mybir.dt.uint32
U8 = mybir.dt.uint8
E4M3X4 = mybir.dt.float8_e4m3fn_x4
E5M2X4 = mybir.dt.float8_e5m2_x4

P = 128
PACK = 4
K_PASS = P * PACK
TOKENS = 1024
H = 1536
N = 512
TOKEN_PASSES = TOKENS // K_PASS
FEATURE_PASSES = H // K_PASS
BLOCKS = H // N
RUN = 4

FLOPS = 2 * 2 * TOKENS * H * H
BYTES = 2 * (2 * TOKENS * H + 2 * H * H) + 4 * (TOKENS * H + H * H)


def tile_neuroplasticitylayer_v_kernel(
    tc, x, plastic_weights, plasticity_rate, fixed_w, fixed_b, hebbian_strength, grad_out, out_0, out_1
):
    nc = tc.nc
    with ExitStack() as ctx:
        keep = ctx.enter_context(tc.tile_pool(name="keep", bufs=1))
        stage = ctx.enter_context(tc.tile_pool(name="stage", bufs=9))
        psum = ctx.enter_context(tc.psum_pool(name="psum", bufs=8))
        ctx.enter_context(tc.manual_schedule())

        def big(slot, shape, dtype):
            return keep.tile(shape, dtype, tag="big%d" % slot, name="big%d" % slot, align_bytes=64)

        def load_pass(rows, slot, pieces=1):
            raw = big(slot, [P, PACK * H], BF16)
            view = rows.rearrange("(p j) w -> p (j w)", j=PACK)
            width = PACK * H // pieces
            for piece in range(pieces):
                cols = slice(piece * width, (piece + 1) * width)
                nc.sync.dma_start(out=raw[:, cols], in_=view[:, cols])
            return raw

        def staged(name):
            return stage.tile([P, PACK * N], BF16, tag="staged", name=name, align_bytes=64)

        def block_of(raw, block):
            return raw[:].rearrange("p (j w) -> p j w", j=PACK)[:, :, block * N:(block + 1) * N]

        def copy(on_scalar, out, in_):
            if on_scalar:
                nc.scalar.copy(out=out, in_=in_)
            else:
                nc.vector.tensor_copy(out=out, in_=in_)

        def interleave(rows, on_scalar=False):
            grouped = staged("grouped")
            copy(
                on_scalar,
                grouped[:].rearrange("p (c i t) -> p c t i", i=RUN, t=PACK),
                rows.rearrange("p t (c i) -> p c t i", i=RUN),
            )
            return grouped

        def quantize(grouped, operand, block):
            codes, scales, fmt = operand
            cols = slice(block * N, (block + 1) * N)
            nc.vector.quantize_mx(out=codes[:, cols].bitcast(fmt), scales=scales[:, cols], in_=grouped[:])

        def scale_tile(name, width):
            return keep.tile([P, width], U8, tag=name, name=name, align_bytes=64)

        def product(passes, m, block, result, on_scalar=True):
            acc = psum.tile([P, N], F32, tag="bank", name="acc")
            m_cols = slice(m * P, (m + 1) * P)
            n_cols = slice(block * N, (block + 1) * N)
            for index, (left, right) in enumerate(passes):
                nc.tensor.matmul_mx(
                    out=acc[:],
                    lhsT=left[0][:, m_cols].bitcast(left[2]),
                    lhsT_scale=left[1][:, m_cols],
                    rhs=right[0][:, n_cols].bitcast(right[2]),
                    rhs_scale=right[1][:, n_cols],
                    start=(index == 0),
                    stop=(index == len(passes) - 1),
                )
            copy(on_scalar, result, acc[:])

        g_raw = [load_pass(grad_out[0], 0, pieces=2), load_pass(grad_out[1], 1)]
        x_raw = [load_pass(x[0], 2), load_pass(x[1], 3)]
        w_raw = {}

        def load_weights(h, slots):
            rows = slice(h * K_PASS, (h + 1) * K_PASS)
            w_raw[h] = (load_pass(fixed_w[rows, :], slots[0]), load_pass(plastic_weights[rows, :], slots[1]))

        load_weights(0, (4, 5))

        identity = keep.tile([P, P], F32, name="identity")
        make_identity(nc, identity[:])

        g_codes = big(6, [P, TOKEN_PASSES * H], U32)
        x_codes = big(7, [P, TOKEN_PASSES * H], U32)
        g_tok = [(g_codes[:, g * H:(g + 1) * H], scale_tile("g_tok_s%d" % g, H), E5M2X4) for g in range(TOKEN_PASSES)]
        x_tok = [(x_codes[:, g * H:(g + 1) * H], scale_tile("x_tok_s%d" % g, H), E4M3X4) for g in range(TOKEN_PASSES)]
        g_feat = [
            (keep.tile([P, TOKENS], U32, name="g_feat%d" % h, align_bytes=64), scale_tile("g_feat_s%d" % h, TOKENS), E5M2X4)
            for h in range(FEATURE_PASSES)
        ]
        w_q = [
            (keep.tile([P, H], U32, name="w_q%d" % h, align_bytes=64), scale_tile("w_q_s%d" % h, H), E4M3X4)
            for h in range(FEATURE_PASSES)
        ]

        def transpose_pass(g):
            words = g_raw[g][:].bitcast(F32)
            grouped = [staged("turned") for h in range(FEATURE_PASSES)]
            for pair in range(2):
                for h in range(FEATURE_PASSES):
                    bank = psum.tile([P, 2, 2, P], F32, tag="bank", name="turn")
                    for a in range(2):
                        first = (2 * pair + a) * (H // 2) + h * (K_PASS // 2)
                        for u in range(2):
                            nc.tensor.transpose(bank[:, a, u, :], words[:, first + u:first + K_PASS // 2:2], identity[:])
                    half = grouped[h][:].bitcast(F32)[:, pair * N:(pair + 1) * N]
                    nc.scalar.copy(
                        out=half.rearrange("p (a r u) -> p a r u", a=2, u=2),
                        in_=bank[:].rearrange("p a u r -> p a r u"),
                    )
            return grouped

        def add_weights(h, block):
            total = staged("total")
            rows = total[:].rearrange("p (j w) -> p j w", j=PACK)
            nc.vector.tensor_add(out=rows, in0=block_of(w_raw[h][0], block), in1=block_of(w_raw[h][1], block))
            return rows

        turned0 = transpose_pass(0)
        g00 = interleave(block_of(g_raw[0], 0))
        g02 = interleave(block_of(g_raw[0], 2))
        g01 = interleave(block_of(g_raw[0], 1), on_scalar=True)
        quantize(g00, g_tok[0], 0)
        g10 = interleave(block_of(g_raw[1], 0))
        turned1 = transpose_pass(1)
        quantize(g02, g_tok[0], 2)
        for h in range(FEATURE_PASSES):
            quantize(turned0[h], g_feat[h], 0)
        quantize(g10, g_tok[1], 0)
        x00 = interleave(block_of(x_raw[0], 0))
        x01 = interleave(block_of(x_raw[0], 1))
        x02 = interleave(block_of(x_raw[0], 2), on_scalar=True)
        quantize(x00, x_tok[0], 0)
        x10 = interleave(block_of(x_raw[1], 0))
        x11 = interleave(block_of(x_raw[1], 1), on_scalar=True)
        quantize(x01, x_tok[0], 1)
        quantize(x10, x_tok[1], 0)
        x12 = interleave(block_of(x_raw[1], 2))
        load_weights(1, (2, 3))
        quantize(x11, x_tok[1], 1)
        quantize(x02, x_tok[0], 2)
        quantize(x12, x_tok[1], 2)
        g11 = interleave(block_of(g_raw[1], 1))
        quantize(g01, g_tok[0], 1)
        g12 = interleave(block_of(g_raw[1], 2))
        load_weights(2, (0, 1))
        quantize(g11, g_tok[1], 1)
        s00 = add_weights(0, 0)
        quantize(g12, g_tok[1], 2)

        dw_passes = list(zip(g_tok, x_tok))
        dw_rows = out_1.rearrange("(q a p) w -> q p a w", a=2, p=P)

        def dw_cols(tile, a, block):
            return tile[:, a * H + block * N:a * H + (block + 1) * N]

        def store_dw(q, tile):
            nc.sync.dma_start(out=dw_rows[q], in_=tile[:].rearrange("p (a w) -> p a w", a=2))

        first = [big(8 + q, [P, 2 * H], F32) for q in range(2)]
        for block in range(BLOCKS):
            for m in range(4):
                product(dw_passes, m, block, dw_cols(first[m // 2], m % 2, block))
        for q in range(2):
            store_dw(q, first[q])

        def dw_pair(q, slot):
            tile = big(slot, [P, 2 * H], F32)
            for a in range(2):
                for block in range(BLOCKS):
                    product(dw_passes, 2 * q + a, block, dw_cols(tile, a, block))
            store_dw(q, tile)

        for q in range(2, 5):
            dw_pair(q, 8 + q)

        w00 = interleave(s00)
        s01 = add_weights(0, 1)
        quantize(w00, w_q[0], 0)
        s02 = add_weights(0, 2)
        dw_pair(5, 4)
        s10 = add_weights(1, 0)
        quantize(turned1[0], g_feat[0], 1)
        w10 = interleave(s10)
        s11 = add_weights(1, 1)
        quantize(w10, w_q[1], 0)
        s20 = add_weights(2, 0)
        quantize(turned1[1], g_feat[1], 1)
        w20 = interleave(s20)
        quantize(turned1[2], g_feat[2], 1)
        quantize(w20, w_q[2], 0)

        dx_passes = list(zip(g_feat, w_q))
        dx_rows = out_0.rearrange("g (p q a) w -> g q p a w", q=2, a=2)
        dx_tiles = [big(5 + pair, [P, 2 * H], F32) for pair in range(4)]

        def dx_block(pair, block, shared=False):
            for a in range(2):
                product(dx_passes, 2 * pair + a, block, dw_cols(dx_tiles[pair], a, block), not shared or a == 0)

        def store_dx(pair, first, last):
            cols = slice(first * N, last * N)
            nc.sync.dma_start(
                out=dx_rows[pair // 2, pair % 2][:, :, cols],
                in_=dx_tiles[pair][:].rearrange("p (a w) -> p a w", a=2)[:, :, cols],
            )

        w01 = interleave(s01, on_scalar=True)
        dx_block(0, 0)
        dx_block(1, 0)
        w02 = interleave(s02, on_scalar=True)
        dx_block(2, 0)
        dx_block(3, 0)
        s21 = add_weights(2, 1)
        w11 = interleave(s11)
        w21 = interleave(s21)
        quantize(w01, w_q[0], 1)
        quantize(w11, w_q[1], 1)
        quantize(w21, w_q[2], 1)
        for pair in range(2):
            dx_block(pair, 1)
            store_dx(pair, 0, 2)
        s12 = add_weights(1, 2)
        s22 = add_weights(2, 2)
        w12 = interleave(s12)
        w22 = interleave(s22)
        quantize(w02, w_q[0], 2)
        quantize(w12, w_q[1], 2)
        quantize(w22, w_q[2], 2)
        for pair in range(2, 4):
            dx_block(pair, 1, shared=pair == 3)
            dx_block(pair, 2, shared=True)
            store_dx(pair, 0, 3)
        for pair in range(2):
            dx_block(pair, 2, shared=True)
            store_dx(pair, 2, 3)
